import numpy as np
import ml_dtypes


def mxq(x, axis, fmt="e4m3"):
    dtype, down = {"e4m3": (ml_dtypes.float8_e4m3fn, 7), "e5m2": (ml_dtypes.float8_e5m2, 14)}[fmt]
    v = np.moveaxis(np.asarray(x, np.float32).astype(ml_dtypes.bfloat16).astype(np.float64), axis, -1)
    blocks = v.reshape(v.shape[:-1] + (-1, 32))
    amax = np.abs(blocks).max(-1, keepdims=True)
    byte = np.maximum(np.where(amax > 0, np.frexp(amax)[1] - 1 + 127, 0) - down, 1)
    scale = np.exp2(byte - 127.0)
    codes = (blocks / scale).astype(np.float32).astype(dtype).astype(np.float64)
    return np.moveaxis((codes * scale).reshape(v.shape), -1, axis)


WIDE = False


def mx_kscale(k):
    if not WIDE:
        return np.ones(k)
    levels = np.array([10, -10, 5, -5, 0])
    if k % 512:
        return np.exp2(np.random.permutation(np.resize(levels, k // 32))).repeat(32)
    a = np.empty((k // 512, 16))
    for p in range(k // 512):
        a[p, :8] = np.random.permutation(np.resize(levels, 8))
        for g in range(8):
            far = levels[np.abs(levels - a[p, g]) >= 10]
            a[p, g + 8] = far[np.random.randint(len(far))]
    return np.exp2(a.ravel()).repeat(32)


BF16 = ml_dtypes.bfloat16


def bf(x):
    return np.asarray(x, np.float32).astype(BF16)


def f64(x):
    return np.asarray(x).astype(np.float64)


B, S, D, L, H, DH = 4, 1024, 1024, 1024, 4, 64
HALF = DH // 2
QW = H * HALF
NF = HALF // 2


def rope_tables():
    inv_freq = 1.0 / (10000.0 ** (np.arange(0, HALF, 2) / HALF))
    freqs = np.arange(S)[:, None] * inv_freq[None, :]
    return np.cos(freqs), np.sin(freqs)


def apply_rope(xr, cos, sin):
    rot, pas = xr[..., :NF], xr[..., NF:]
    c = cos[None, :, None, :]
    s = sin[None, :, None, :]
    return np.concatenate([rot * c - pas * s, rot * s + pas * c], axis=-1)


def draw0():
    s, t = mx_kscale(D), mx_kscale(L)
    return {"x": bf(np.random.standard_normal((B, S, D)) * s),
            "W_q_d": bf(np.random.standard_normal((D, L)) / np.sqrt(D) / s[:, None] * t),
            "b_q_d": bf(np.random.standard_normal(L) * 0.3 * t),
            "W_q_u": bf(np.random.standard_normal((L, QW)) / np.sqrt(L) / t[:, None]),
            "b_q_u": bf(np.random.standard_normal(QW) * 0.3),
            "W_rq": bf(np.random.standard_normal((L, QW)) / np.sqrt(L) / t[:, None]),
            "b_rq": bf(np.random.standard_normal(QW) * 0.3)}


def core(x, W_q_d, b_q_d, W_q_u, b_q_u, W_rq, b_rq):
    cos, sin = rope_tables()
    q_d = (mxq(f64(x), 2, "e4m3") @ mxq(f64(W_q_d), 0, "e4m3")) + f64(b_q_d)
    qdq = mxq(q_d, 2, "e4m3")
    q1 = ((qdq @ mxq(f64(W_q_u), 0, "e4m3")) + f64(b_q_u)).reshape(B, S, H, HALF)
    q2 = ((qdq @ mxq(f64(W_rq), 0, "e4m3")) + f64(b_rq)).reshape(B, S, H, HALF)
    q2 = apply_rope(q2, cos, sin)
    return np.concatenate([q1, q2], axis=-1)


def e4m3fn_bytes(y):
    return np.clip(np.asarray(y, np.float64), -448.0, 448.0).astype(np.float32).astype(ml_dtypes.float8_e4m3fn).view(np.uint8)


def e4m3fn_values(b):
    return np.asarray(b, np.uint8).view(ml_dtypes.float8_e4m3fn).astype(np.float64)


def setup_inputs():
    d = draw0()
    x0 = np.asarray(d['x']).astype(np.float64)
    s = (np.max(np.abs(x0), axis=(0, 1), keepdims=True) / 448.0).astype(np.float32)
    out = {}
    for k, v in d.items():
        if k == 'x':
            out['x_bytes'] = e4m3fn_bytes(x0 / s.astype(np.float64))
            out['x_scale'] = s
        else:
            out[k] = v
    return out


def reference(x_bytes, x_scale, W_q_d, b_q_d, W_q_u, b_q_u, W_rq, b_rq):
    return core(e4m3fn_values(x_bytes) * x_scale.astype(np.float64), W_q_d, b_q_d, W_q_u, b_q_u, W_rq, b_rq)

@@ -1,0 +1,306 @@
+import math
+from contextlib import ExitStack
+
+import concourse.mybir as mybir
+from concourse.masks import make_identity
+
+F32 = mybir.dt.float32
+BF16 = mybir.dt.bfloat16
+I32 = mybir.dt.int32
+U32 = mybir.dt.uint32
+U8 = mybir.dt.uint8
+FP8 = mybir.dt.float8_e4m3fn
+FP8X4 = mybir.dt.float8_e4m3fn_x4
+ACT = mybir.ActivationFunctionType
+ALU = mybir.AluOpType
+
+P = 128
+B, S, D, L = 4, 1024, 1024, 1024
+H, HALF = 4, 32
+NF = HALF // 2
+QW = H * HALF
+PACK = 4
+K_PASS = P * PACK
+G = D // K_PASS
+TOK = 512
+SUB = TOK // P
+TILES = B * S // TOK
+FLOPS = 2 * B * S * D * L + 2 * B * S * L * 2 * QW
+
+
+def tile_multiheadlatentattention_pa_t_kernel(
+    tc, x_bytes, x_scale, W_q_d, b_q_d, W_q_u, b_q_u, W_rq, b_rq, out
+):
+    nc = tc.nc
+    x_rows = x_bytes.rearrange("b (i p a) k -> (b i) p a k", p=P, a=SUB)
+    out_rows = out.rearrange("b (i p a) h d -> (b i) p a (h d)", p=P, a=SUB)
+
+    with ExitStack() as ctx:
+        keep = ctx.enter_context(tc.tile_pool(name="keep", bufs=1))
+        work = ctx.enter_context(tc.tile_pool(name="work", bufs=2))
+        psum = ctx.enter_context(tc.psum_pool(name="psum", bufs=1))
+        ctx.enter_context(tc.manual_schedule())
+
+        scale = keep.tile([P, D], F32, name="scale")
+        nc.scalar.dma_start(out=scale[:], in_=x_scale.rearrange("o u k -> (o u k)").partition_broadcast(P))
+        xb = [keep.tile([P, SUB, D], U8, name=f"xb{i}") for i in range(TILES)]
+        nc.sync.dma_start(out=xb[0][:, 0:2, :], in_=x_rows[0][:, 0:2, :])
+        nc.sync.dma_start(out=xb[0][:, 2:4, :], in_=x_rows[0][:, 2:4, :])
+        w_raw = {}
+        for g2 in range(G):
+            for g in range(G):
+                w_raw[g, g2] = keep.tile([P, PACK, K_PASS], BF16, name=f"wraw{g}{g2}")
+                nc.sync.dma_start(
+                    out=w_raw[g, g2][:],
+                    in_=W_q_d[g * K_PASS : (g + 1) * K_PASS, g2 * K_PASS : (g2 + 1) * K_PASS].rearrange("(p j) c -> p j c", j=PACK),
+                )
+        nc.sync.dma_start(out=xb[1][:], in_=x_rows[1])
+        w2_raw = keep.tile([P, 2, G, PACK, QW], BF16, name="w2raw")
+        for s, w in enumerate((W_q_u, W_rq)):
+            for g in range(G):
+                nc.sync.dma_start(out=w2_raw[:, s, g, :, :], in_=w[g * K_PASS : (g + 1) * K_PASS, :].rearrange("(p j) c -> p j c", j=PACK))
+        for i in range(2, TILES):
+            nc.sync.dma_start(out=xb[i][:], in_=x_rows[i])
+
+        bd16 = keep.tile([P, G, PACK], BF16, name="bd16")
+        bu16 = keep.tile([P, 1], BF16, name="bu16")
+        br16 = keep.tile([P, 1], BF16, name="br16")
+        nc.gpsimd.dma_start(out=bd16[:], in_=b_q_d.rearrange("(g p t) -> p g t", p=P, t=PACK))
+        nc.gpsimd.dma_start(out=bu16[:], in_=b_q_u.rearrange("(p o) -> p o", o=1))
+        nc.gpsimd.dma_start(out=br16[:], in_=b_rq.rearrange("(p o) -> p o", o=1))
+
+        ident = keep.tile([P, P], F32, name="ident")
+        make_identity(nc, ident[:])
+        swap = keep.tile([P, H, 2, NF], F32, name="swap")
+        ident_h = ident[:].rearrange("p (h e j) -> p h e j", h=H, e=2)
+        nc.gpsimd.tensor_copy(out=swap[:, :, 0, :], in_=ident_h[:, :, 1, :])
+        nc.gpsimd.tensor_copy(out=swap[:, :, 1, :], in_=ident_h[:, :, 0, :])
+
+        zero = keep.tile([P, H], F32, name="zero")
+        nc.gpsimd.memset(zero[:], 0.0)
+        turn_row = keep.tile([P, H, 2, NF], F32, name="turn_row")
+        for j in range(NF):
+            nc.gpsimd.tensor_scalar(
+                out=turn_row[:, :, 0, j], in0=zero[:], scalar1=10000.0 ** (-j / NF) / (2.0 * math.pi), scalar2=None, op0=ALU.add
+            )
+        nc.gpsimd.tensor_scalar(out=turn_row[:, :, 1, :], in0=turn_row[:, :, 0, :], scalar1=-1.0, scalar2=None, op0=ALU.mult)
+        pos = keep.tile([P, S], F32, name="pos")
+        nc.gpsimd.iota(
+            pos[:].rearrange("p (i a q) -> p i a q", a=SUB, q=P),
+            pattern=[[TOK, S // TOK], [1, SUB], [SUB, P]],
+            base=0,
+            channel_multiplier=0,
+            allow_small_or_imprecise_dtypes=True,
+        )
+        bd = keep.tile([P, G, PACK], F32, name="bd")
+        bu = keep.tile([P, 1], F32, name="bu")
+        br = keep.tile([P, 1], F32, name="br")
+        nc.gpsimd.tensor_copy(out=bd[:], in_=bd16[:])
+        nc.gpsimd.tensor_copy(out=bu[:], in_=bu16[:])
+        nc.gpsimd.tensor_copy(out=br[:], in_=br16[:])
+
+        xs, xg, xq, xqs = {}, {}, {}, {}
+        wg, wq, wqs = {}, {}, {}
+        qp, qg, qq, qqs = {}, {}, {}, {}
+        acc2, o1, m1, m2, osb = {}, {}, {}, {}, {}
+
+        def product(i, a):
+            xs[i, a] = work.tile([P, D], BF16, name="xs", bufs=6, align_bytes=64)
+            nc.vector.tensor_tensor(out=xs[i, a][:], in0=xb[i][:, a, :].bitcast(FP8), in1=scale[:], op=ALU.mult)
+
+        def turn(i, a):
+            bank = psum.tile([P, G, 2, P], F32, name="tp", bufs=3)
+            words = xs[i, a][:].bitcast(F32)
+            for g in range(G):
+                for u in range(2):
+                    nc.tensor.transpose(bank[:, g, u, :], words[:, 256 * g + u : 256 * (g + 1) : 2], ident[:])
+            if a == 0:
+                xg[i] = work.tile([P, G, TOK, PACK], BF16, name="xg", align_bytes=64)
+            dst = xg[i][:].rearrange("p g n t -> p (g n t)").bitcast(F32).rearrange("p (g n u) -> p g n u", g=G, u=2)
+            nc.scalar.copy(out=dst[:, :, a * P : (a + 1) * P, :], in_=bank[:].rearrange("p g u r -> p g r u"))
+
+        def quantize_x(i, g):
+            if g == 0:
+                xq[i] = work.tile([P, G, TOK], U32, name="xq", align_bytes=64)
+                xqs[i] = work.tile([P, G, TOK], U8, name="xqs", align_bytes=64)
+            nc.vector.quantize_mx(
+                out=xq[i][:, g, :].bitcast(FP8X4), scales=xqs[i][:, g, :], in_=xg[i][:, g, :, :].rearrange("p n t -> p (n t)")
+            )
+
+        def group_w(g, g2, copy):
+            wg[g, g2] = keep.tile([P, K_PASS, PACK], BF16, name=f"wg{g}{g2}", align_bytes=64)
+            copy(
+                out=wg[g, g2][:].rearrange("p (t m) j -> p t m j", t=PACK),
+                in_=w_raw[g, g2][:].rearrange("p j (m t) -> p t m j", t=PACK),
+            )
+
+        def quantize_w(g, g2):
+            wq[g, g2] = keep.tile([P, K_PASS], U32, name=f"wq{g}{g2}", align_bytes=64)
+            wqs[g, g2] = keep.tile([P, K_PASS], U8, name=f"wqs{g}{g2}", align_bytes=64)
+            nc.vector.quantize_mx(
+                out=wq[g, g2][:].bitcast(FP8X4), scales=wqs[g, g2][:], in_=wg[g, g2][:].rearrange("p n j -> p (n j)")
+            )
+
+        w2g = keep.tile([P, 2, G, QW, PACK], BF16, name="w2g", align_bytes=64)
+        w2q = keep.tile([P, 2, G, QW], U32, name="w2q", align_bytes=64)
+        w2qs = keep.tile([P, 2, G, QW], U8, name="w2qs", align_bytes=64)
+
+        def latent(i, g2):
+            qp[i, g2] = work.tile([P, PACK, TOK], BF16, name="qp", bufs=3, align_bytes=64)
+            for t in range(PACK):
+                bank = psum.tile([P, TOK], F32, name="s1", bufs=3)
+                for g in range(G):
+                    nc.tensor.matmul_mx(
+                        out=bank[:],
+                        lhsT=wq[g, g2][:, t * P : (t + 1) * P].bitcast(FP8X4),
+                        lhsT_scale=wqs[g, g2][:, t * P : (t + 1) * P],
+                        rhs=xq[i][:, g, :].bitcast(FP8X4),
+                        rhs_scale=xqs[i][:, g, :],
+                        start=(g == 0),
+                        stop=(g == G - 1),
+                    )
+                nc.scalar.activation(out=qp[i, g2][:, t, :], in_=bank[:], func=ACT.Identity, bias=bd[:, g2, t : t + 1])
+
+        def group_q(i, g2):
+            qg[i, g2] = work.tile([P, TOK, PACK], BF16, name="qg", bufs=3, align_bytes=64)
+            nc.vector.tensor_copy(
+                out=qg[i, g2][:].rearrange("p (c n) t -> p c t n", n=4), in_=qp[i, g2][:].rearrange("p t (c n) -> p c t n", n=4)
+            )
+
+        def quantize_q(i, g2):
+            if g2 == 0:
+                qq[i] = work.tile([P, G, TOK], U32, name="qq", align_bytes=64)
+                qqs[i] = work.tile([P, G, TOK], U8, name="qqs", align_bytes=64)
+            nc.vector.quantize_mx(
+                out=qq[i][:, g2, :].bitcast(FP8X4), scales=qqs[i][:, g2, :], in_=qg[i, g2][:].rearrange("p n t -> p (n t)")
+            )
+
+        def heads(i):
+            for s in range(2):
+                acc2[i, s] = psum.tile([P, TOK], F32, name=f"s2{s}")
+                for g in range(G):
+                    nc.tensor.matmul_mx(
+                        out=acc2[i, s][:],
+                        lhsT=w2q[:, s, g, :].bitcast(FP8X4),
+                        lhsT_scale=w2qs[:, s, g, :],
+                        rhs=qq[i][:, g, :].bitcast(FP8X4),
+                        rhs_scale=qqs[i][:, g, :],
+                        start=(g == 0),
+                        stop=(g == G - 1),
+                    )
+
+        def head1(i):
+            o1[i] = work.tile([P, TOK], F32, name="o1")
+            nc.scalar.activation(out=o1[i][:], in_=acc2[i, 0][:], func=ACT.Identity, bias=bu[:])
+
+        def rope(i):
+            cols = slice((i % 2) * TOK, (i % 2 + 1) * TOK)
+            m1[i] = work.tile([P, TOK], F32, name="m1")
+            m2[i] = work.tile([P, TOK], F32, name="m2")
+            nc.vector.scalar_tensor_tensor(out=m1[i][:], in0=acc2[i, 1][:], scalar=br[:], in1=cos[:, cols], op0=ALU.add, op1=ALU.mult)
+            nc.vector.scalar_tensor_tensor(out=m2[i][:], in0=acc2[i, 1][:], scalar=br[:], in1=sin[:, cols], op0=ALU.add, op1=ALU.mult)
+
+        def finish(i):
+            osb[i] = work.tile([P, SUB, 2 * QW], F32, name="osb")
+            for half in range(2):
+                bank = psum.tile([P, 2, 2 * QW], F32, name="tp", bufs=3)
+                for r in range(2):
+                    a = 2 * half + r
+                    cols = slice(a * P, (a + 1) * P)
+                    nc.tensor.transpose(bank[:, r, 0:QW], o1[i][:, cols], ident[:])
+                    nc.tensor.matmul(bank[:, r, QW : 2 * QW], lhsT=m1[i][:, cols], rhs=ident[:], start=True, stop=False, is_transpose=True)
+                    nc.tensor.matmul(
+                        bank[:, r, QW : 2 * QW],
+                        lhsT=m2[i][:, cols],
+                        rhs=swap[:].rearrange("p h e j -> p (h e j)"),
+                        start=False,
+                        stop=True,
+                        is_transpose=True,
+                    )
+                nc.scalar.copy(
+                    out=osb[i][:, 2 * half : 2 * half + 2, :].rearrange("p r (h s d) -> p r s h d", h=H, s=2),
+                    in_=bank[:].rearrange("p r (s h d) -> p r s h d", s=2, h=H),
+                )
+                nc.sync.dma_start(out=out_rows[i][:, 2 * half : 2 * half + 2, :], in_=osb[i][:, 2 * half : 2 * half + 2, :])
+
+        for a in range(SUB):
+            product(0, a)
+        group_w(0, 0, nc.scalar.copy)
+        group_w(1, 0, nc.vector.tensor_copy)
+        for a in range(SUB):
+            turn(0, a)
+        quantize_w(0, 0)
+        quantize_w(1, 0)
+        quantize_x(0, 0)
+        quantize_x(0, 1)
+        group_w(0, 1, nc.scalar.copy)
+        group_w(1, 1, nc.vector.tensor_copy)
+        quantize_w(0, 1)
+        quantize_w(1, 1)
+        product(1, 0)
+        product(1, 1)
+        nc.vector.tensor_copy(
+            out=w2g[:].rearrange("p s g n j -> p (s g) n j"), in_=w2_raw[:].rearrange("p s g j n -> p (s g) n j")
+        )
+        product(1, 2)
+        nc.vector.quantize_mx(
+            out=w2q[:].rearrange("p s g n -> p (s g n)").bitcast(FP8X4),
+            scales=w2qs[:].rearrange("p s g n -> p (s g n)"),
+            in_=w2g[:].rearrange("p s g n j -> p (s g n j)"),
+        )
+        product(1, 3)
+
+        freq_bank = psum.tile([P, P], F32, name="s20")
+        nc.tensor.transpose(freq_bank[:], turn_row[:].rearrange("p h e j -> p (h e j)"), ident[:])
+        freq = keep.tile([P, 1], F32, name="freq")
+        nc.scalar.copy(out=freq[:], in_=freq_bank[:, 0:1])
+        turns = keep.tile([P, S], F32, name="turns")
+        whole = keep.tile([P, S], I32, name="whole")
+        frac = keep.tile([P, S], F32, name="frac")
+        sin = keep.tile([P, S], F32, name="sin")
+        cos = keep.tile([P, S], F32, name="cos")
+        half_sin = keep.tile([P, S], F32, name="half_sin")
+        nc.gpsimd.tensor_scalar(out=turns[:], in0=pos[:], scalar1=freq[:], scalar2=None, op0=ALU.mult)
+        nc.vector.tensor_copy(out=whole[:], in_=turns[:])
+        nc.vector.scalar_tensor_tensor(out=frac[:], in0=whole[:], scalar=-1.0, in1=turns[:], op0=ALU.mult, op1=ALU.add)
+        nc.scalar.activation(out=sin[:], in_=frac[:], func=ACT.Sin, scale=2.0 * math.pi)
+        nc.scalar.activation(out=half_sin[:], in_=frac[:], func=ACT.Sin, scale=math.pi)
+        nc.gpsimd.tensor_tensor(out=cos[:], in0=half_sin[:], in1=half_sin[:], op=ALU.mult)
+        nc.gpsimd.tensor_scalar(out=cos[:], in0=cos[:], scalar1=-2.0, scalar2=1.0, op0=ALU.mult, op1=ALU.add)
+
+        for i in range(TILES + 2):
+            ahead = i + 2 < TILES
+            latent_on = i < TILES
+            head_on = 1 <= i <= TILES
+            if latent_on:
+                latent(i, 0)
+            if head_on:
+                group_q(i - 1, 1)
+            if ahead:
+                product(i + 2, 0)
+            if head_on:
+                quantize_q(i - 1, 1)
+            if ahead:
+                product(i + 2, 1)
+            if i >= 2:
+                finish(i - 2)
+            if latent_on:
+                group_q(i, 0)
+            if ahead:
+                product(i + 2, 2)
+            if i + 1 < TILES:
+                for a in range(SUB):
+                    turn(i + 1, a)
+            if latent_on:
+                quantize_q(i, 0)
+            if ahead:
+                product(i + 2, 3)
+            if latent_on:
+                latent(i, 1)
+            if i + 1 < TILES:
+                quantize_x(i + 1, 0)
+                quantize_x(i + 1, 1)
+            if head_on:
+                heads(i - 1)
+                head1(i - 1)
+                rope(i - 1)

@@ -145,9 +145,10 @@ def tile_multiheadlatentattention_pa_t_kernel(
         w2q = keep.tile([P, 2, G, QW], U32, name="w2q", align_bytes=64)
         w2qs = keep.tile([P, 2, G, QW], U8, name="w2qs", align_bytes=64)
 
-        def latent(i, g2):
-            qp[i, g2] = work.tile([P, PACK, TOK], BF16, name="qp", bufs=3, align_bytes=64)
-            for t in range(PACK):
+        def latent(i, g2, slots):
+            if slots[0] == 0:
+                qp[i, g2] = work.tile([P, PACK, TOK], BF16, name="qp", bufs=3, align_bytes=64)
+            for t in slots:
                 bank = psum.tile([P, TOK], F32, name="s1", bufs=3)
                 for g in range(G):
                     nc.tensor.matmul_mx(
@@ -260,7 +261,7 @@ def tile_multiheadlatentattention_pa_t_kernel(
         sin = keep.tile([P, S], F32, name="sin")
         cos = keep.tile([P, S], F32, name="cos")
         half_sin = keep.tile([P, S], F32, name="half_sin")
-        nc.gpsimd.tensor_scalar(out=turns[:], in0=pos[:], scalar1=freq[:], scalar2=None, op0=ALU.mult)
+        nc.scalar.activation(out=turns[:], in_=pos[:], func=ACT.Copy, scale=freq[:])
         nc.vector.tensor_copy(out=whole[:], in_=turns[:])
         nc.vector.scalar_tensor_tensor(out=frac[:], in0=whole[:], scalar=-1.0, in1=turns[:], op0=ALU.mult, op1=ALU.add)
         nc.scalar.activation(out=sin[:], in_=frac[:], func=ACT.Sin, scale=2.0 * math.pi)
@@ -270,34 +271,40 @@ def tile_multiheadlatentattention_pa_t_kernel(
 
         for i in range(TILES + 2):
             ahead = i + 2 < TILES
+            turn_on = i + 1 < TILES
             latent_on = i < TILES
             head_on = 1 <= i <= TILES
             if latent_on:
-                latent(i, 0)
-            if head_on:
-                group_q(i - 1, 1)
+                latent(i, 0, (0, 1))
             if ahead:
                 product(i + 2, 0)
+            if turn_on:
+                turn(i + 1, 0)
+                turn(i + 1, 1)
+            if head_on:
+                group_q(i - 1, 1)
+            if latent_on:
+                latent(i, 0, (2, 3))
+            if ahead:
+                product(i + 2, 1)
+            if turn_on:
+                turn(i + 1, 2)
+                turn(i + 1, 3)
             if head_on:
                 quantize_q(i - 1, 1)
             if ahead:
-                product(i + 2, 1)
+                product(i + 2, 2)
+            if latent_on:
+                latent(i, 1, (0, 1))
+                group_q(i, 0)
             if i >= 2:
                 finish(i - 2)
-            if latent_on:
-                group_q(i, 0)
-            if ahead:
-                product(i + 2, 2)
-            if i + 1 < TILES:
-                for a in range(SUB):
-                    turn(i + 1, a)
-            if latent_on:
-                quantize_q(i, 0)
             if ahead:
                 product(i + 2, 3)
             if latent_on:
-                latent(i, 1)
-            if i + 1 < TILES:
+                quantize_q(i, 0)
+                latent(i, 1, (2, 3))
+            if turn_on:
                 quantize_x(i + 1, 0)
                 quantize_x(i + 1, 1)
             if head_on:

@@ -41,8 +41,8 @@ def tile_multiheadlatentattention_pa_t_kernel(
         psum = ctx.enter_context(tc.psum_pool(name="psum", bufs=1))
         ctx.enter_context(tc.manual_schedule())
 
-        scale = keep.tile([P, D], F32, name="scale")
-        nc.scalar.dma_start(out=scale[:], in_=x_scale.rearrange("o u k -> (o u k)").partition_broadcast(P))
+        scale = keep.tile([P, G, PACK], F32, name="scale")
+        nc.scalar.dma_start(out=scale[:], in_=x_scale.rearrange("o u (g p t) -> p (o u g) t", p=P, t=PACK))
         xb = [keep.tile([P, SUB, D], U8, name=f"xb{i}") for i in range(TILES)]
         nc.sync.dma_start(out=xb[0][:, 0:2, :], in_=x_rows[0][:, 0:2, :])
         nc.sync.dma_start(out=xb[0][:, 2:4, :], in_=x_rows[0][:, 2:4, :])
@@ -99,25 +99,35 @@ def tile_multiheadlatentattention_pa_t_kernel(
         nc.gpsimd.tensor_copy(out=bu[:], in_=bu16[:])
         nc.gpsimd.tensor_copy(out=br[:], in_=br16[:])
 
-        xs, xg, xq, xqs = {}, {}, {}, {}
+        xs, xt, xg, xq, xqs = {}, {}, {}, {}, {}
         wg, wq, wqs = {}, {}, {}
         qp, qg, qq, qqs = {}, {}, {}, {}
         acc2, o1, m1, m2, osb = {}, {}, {}, {}, {}
 
-        def product(i, a):
-            xs[i, a] = work.tile([P, D], BF16, name="xs", bufs=6, align_bytes=64)
-            nc.vector.tensor_tensor(out=xs[i, a][:], in0=xb[i][:, a, :].bitcast(FP8), in1=scale[:], op=ALU.mult)
+        def widen(i, part):
+            if part == 0:
+                xs[i] = work.tile([P, SUB, D], BF16, name="xs", bufs=3, align_bytes=64)
+            two = slice(2 * part, 2 * part + 2)
+            nc.scalar.copy(out=xs[i][:, two, :], in_=xb[i][:, two, :].bitcast(FP8))
 
         def turn(i, a):
-            bank = psum.tile([P, G, 2, P], F32, name="tp", bufs=3)
-            words = xs[i, a][:].bitcast(F32)
+            xt[i, a] = psum.tile([P, G, 2, P], F32, name="tp", bufs=3)
+            words = xs[i][:, a, :].bitcast(F32)
             for g in range(G):
                 for u in range(2):
-                    nc.tensor.transpose(bank[:, g, u, :], words[:, 256 * g + u : 256 * (g + 1) : 2], ident[:])
+                    nc.tensor.transpose(xt[i, a][:, g, u, :], words[:, 256 * g + u : 256 * (g + 1) : 2], ident[:])
+
+        def product(i, a):
             if a == 0:
                 xg[i] = work.tile([P, G, TOK, PACK], BF16, name="xg", align_bytes=64)
-            dst = xg[i][:].rearrange("p g n t -> p (g n t)").bitcast(F32).rearrange("p (g n u) -> p g n u", g=G, u=2)
-            nc.scalar.copy(out=dst[:, :, a * P : (a + 1) * P, :], in_=bank[:].rearrange("p g u r -> p g r u"))
+            halves = xt[i, a][:].rearrange("p g u r -> p (g u r)").bitcast(BF16)
+            for g in range(G):
+                nc.vector.tensor_tensor(
+                    out=xg[i][:, g, a * P : (a + 1) * P, :].rearrange("p r (u e) -> p r u e", e=2),
+                    in0=halves[:, g * 512 : (g + 1) * 512].rearrange("p (u r e) -> p r u e", u=2, e=2),
+                    in1=scale[:, g : g + 1, :].to_broadcast([P, P, PACK]).rearrange("p r (u e) -> p r u e", e=2),
+                    op=ALU.mult,
+                )
 
         def quantize_x(i, g):
             if g == 0:
@@ -127,12 +137,14 @@ def tile_multiheadlatentattention_pa_t_kernel(
                 out=xq[i][:, g, :].bitcast(FP8X4), scales=xqs[i][:, g, :], in_=xg[i][:, g, :, :].rearrange("p n t -> p (n t)")
             )
 
-        def group_w(g, g2, copy):
+        def group_w(g, g2, on_scalar):
             wg[g, g2] = keep.tile([P, K_PASS, PACK], BF16, name=f"wg{g}{g2}", align_bytes=64)
-            copy(
-                out=wg[g, g2][:].rearrange("p (t m) j -> p t m j", t=PACK),
-                in_=w_raw[g, g2][:].rearrange("p j (m t) -> p t m j", t=PACK),
-            )
+            dst = wg[g, g2][:].rearrange("p (t m) j -> p t m j", t=PACK)
+            rows = w_raw[g, g2][:].rearrange("p j (m t) -> p t m j", t=PACK)
+            if on_scalar:
+                nc.scalar.copy(out=dst, in_=rows)
+            else:
+                nc.vector.tensor_copy(out=dst, in_=rows)
 
         def quantize_w(g, g2):
             wq[g, g2] = keep.tile([P, K_PASS], U32, name=f"wq{g}{g2}", align_bytes=64)
@@ -224,32 +236,30 @@ def tile_multiheadlatentattention_pa_t_kernel(
                 )
                 nc.sync.dma_start(out=out_rows[i][:, 2 * half : 2 * half + 2, :], in_=osb[i][:, 2 * half : 2 * half + 2, :])
 
-        for a in range(SUB):
-            product(0, a)
-        group_w(0, 0, nc.scalar.copy)
-        group_w(1, 0, nc.vector.tensor_copy)
-        for a in range(SUB):
+        widen(0, 0)
+        widen(0, 1)
+        group_w(0, 0, True)
+        for a in range(3):
             turn(0, a)
+        product(0, 0)
+        product(0, 1)
+        turn(0, 3)
+        group_w(1, 0, False)
+        product(0, 2)
         quantize_w(0, 0)
+        product(0, 3)
         quantize_w(1, 0)
         quantize_x(0, 0)
         quantize_x(0, 1)
-        group_w(0, 1, nc.scalar.copy)
-        group_w(1, 1, nc.vector.tensor_copy)
+        group_w(0, 1, True)
+        group_w(1, 1, False)
+        widen(1, 0)
+        widen(1, 1)
         quantize_w(0, 1)
         quantize_w(1, 1)
-        product(1, 0)
-        product(1, 1)
         nc.vector.tensor_copy(
             out=w2g[:].rearrange("p s g n j -> p (s g) n j"), in_=w2_raw[:].rearrange("p s g j n -> p (s g) n j")
         )
-        product(1, 2)
-        nc.vector.quantize_mx(
-            out=w2q[:].rearrange("p s g n -> p (s g n)").bitcast(FP8X4),
-            scales=w2qs[:].rearrange("p s g n -> p (s g n)"),
-            in_=w2g[:].rearrange("p s g n j -> p (s g n j)"),
-        )
-        product(1, 3)
 
         freq_bank = psum.tile([P, P], F32, name="s20")
         nc.tensor.transpose(freq_bank[:], turn_row[:].rearrange("p h e j -> p (h e j)"), ident[:])
@@ -269,6 +279,12 @@ def tile_multiheadlatentattention_pa_t_kernel(
         nc.gpsimd.tensor_tensor(out=cos[:], in0=half_sin[:], in1=half_sin[:], op=ALU.mult)
         nc.gpsimd.tensor_scalar(out=cos[:], in0=cos[:], scalar1=-2.0, scalar2=1.0, op0=ALU.mult, op1=ALU.add)
 
+        nc.vector.quantize_mx(
+            out=w2q[:].rearrange("p s g n -> p (s g n)").bitcast(FP8X4),
+            scales=w2qs[:].rearrange("p s g n -> p (s g n)"),
+            in_=w2g[:].rearrange("p s g n j -> p (s g n j)"),
+        )
+
         for i in range(TILES + 2):
             ahead = i + 2 < TILES
             turn_on = i + 1 < TILES
@@ -276,31 +292,33 @@ def tile_multiheadlatentattention_pa_t_kernel(
             head_on = 1 <= i <= TILES
             if latent_on:
                 latent(i, 0, (0, 1))
-            if ahead:
-                product(i + 2, 0)
             if turn_on:
                 turn(i + 1, 0)
                 turn(i + 1, 1)
+                product(i + 1, 0)
             if head_on:
                 group_q(i - 1, 1)
             if latent_on:
                 latent(i, 0, (2, 3))
-            if ahead:
-                product(i + 2, 1)
             if turn_on:
+                product(i + 1, 1)
                 turn(i + 1, 2)
                 turn(i + 1, 3)
             if head_on:
                 quantize_q(i - 1, 1)
             if ahead:
-                product(i + 2, 2)
+                widen(i + 2, 0)
+            if turn_on:
+                product(i + 1, 2)
             if latent_on:
                 latent(i, 1, (0, 1))
                 group_q(i, 0)
+            if turn_on:
+                product(i + 1, 3)
             if i >= 2:
                 finish(i - 2)
             if ahead:
-                product(i + 2, 3)
+                widen(i + 2, 1)
             if latent_on:
                 quantize_q(i, 0)
                 latent(i, 1, (2, 3))

@@ -24,7 +24,8 @@ K_PASS = P * PACK
 G = D // K_PASS
 TOK = 512
 SUB = TOK // P
-TILES = B * S // TOK
+BLOCKS = B * S // TOK
+TILES = [(0, 0, 2), (0, 2, 2)] + [(i, 0, SUB) for i in range(1, BLOCKS - 1)] + [(BLOCKS - 1, 0, 2), (BLOCKS - 1, 2, 2)]
 FLOPS = 2 * B * S * D * L + 2 * B * S * L * 2 * QW
 
 
@@ -41,11 +42,10 @@ def tile_multiheadlatentattention_pa_t_kernel(
         psum = ctx.enter_context(tc.psum_pool(name="psum", bufs=1))
         ctx.enter_context(tc.manual_schedule())
 
-        scale = keep.tile([P, G, PACK], F32, name="scale")
-        nc.scalar.dma_start(out=scale[:], in_=x_scale.rearrange("o u (g p t) -> p (o u g) t", p=P, t=PACK))
-        xb = [keep.tile([P, SUB, D], U8, name=f"xb{i}") for i in range(TILES)]
+        scale_col = keep.tile([P, D // P], F32, name="scale_col")
+        nc.sync.dma_start(out=scale_col[:], in_=x_scale.rearrange("o u (n c) -> n (o u c)", n=P))
+        xb = [keep.tile([P, SUB, D], U8, name=f"xb{i}") for i in range(BLOCKS)]
         nc.sync.dma_start(out=xb[0][:, 0:2, :], in_=x_rows[0][:, 0:2, :])
-        nc.sync.dma_start(out=xb[0][:, 2:4, :], in_=x_rows[0][:, 2:4, :])
         w_raw = {}
         for g2 in range(G):
             for g in range(G):
@@ -54,20 +54,22 @@ def tile_multiheadlatentattention_pa_t_kernel(
                     out=w_raw[g, g2][:],
                     in_=W_q_d[g * K_PASS : (g + 1) * K_PASS, g2 * K_PASS : (g2 + 1) * K_PASS].rearrange("(p j) c -> p j c", j=PACK),
                 )
+            if g2 == 0:
+                nc.sync.dma_start(out=xb[0][:, 2:4, :], in_=x_rows[0][:, 2:4, :])
         nc.sync.dma_start(out=xb[1][:], in_=x_rows[1])
         w2_raw = keep.tile([P, 2, G, PACK, QW], BF16, name="w2raw")
         for s, w in enumerate((W_q_u, W_rq)):
             for g in range(G):
                 nc.sync.dma_start(out=w2_raw[:, s, g, :, :], in_=w[g * K_PASS : (g + 1) * K_PASS, :].rearrange("(p j) c -> p j c", j=PACK))
-        for i in range(2, TILES):
+        for i in range(2, BLOCKS):
             nc.sync.dma_start(out=xb[i][:], in_=x_rows[i])
 
         bd16 = keep.tile([P, G, PACK], BF16, name="bd16")
         bu16 = keep.tile([P, 1], BF16, name="bu16")
         br16 = keep.tile([P, 1], BF16, name="br16")
-        nc.gpsimd.dma_start(out=bd16[:], in_=b_q_d.rearrange("(g p t) -> p g t", p=P, t=PACK))
-        nc.gpsimd.dma_start(out=bu16[:], in_=b_q_u.rearrange("(p o) -> p o", o=1))
-        nc.gpsimd.dma_start(out=br16[:], in_=b_rq.rearrange("(p o) -> p o", o=1))
+        nc.scalar.dma_start(out=bd16[:], in_=b_q_d.rearrange("(g p t) -> p g t", p=P, t=PACK))
+        nc.scalar.dma_start(out=bu16[:], in_=b_q_u.rearrange("(p o) -> p o", o=1))
+        nc.scalar.dma_start(out=br16[:], in_=b_rq.rearrange("(p o) -> p o", o=1))
 
         ident = keep.tile([P, P], F32, name="ident")
         make_identity(nc, ident[:])
@@ -76,22 +78,22 @@ def tile_multiheadlatentattention_pa_t_kernel(
         nc.gpsimd.tensor_copy(out=swap[:, :, 0, :], in_=ident_h[:, :, 1, :])
         nc.gpsimd.tensor_copy(out=swap[:, :, 1, :], in_=ident_h[:, :, 0, :])
 
-        zero = keep.tile([P, H], F32, name="zero")
-        nc.gpsimd.memset(zero[:], 0.0)
-        turn_row = keep.tile([P, H, 2, NF], F32, name="turn_row")
-        for j in range(NF):
-            nc.gpsimd.tensor_scalar(
-                out=turn_row[:, :, 0, j], in0=zero[:], scalar1=10000.0 ** (-j / NF) / (2.0 * math.pi), scalar2=None, op0=ALU.add
-            )
-        nc.gpsimd.tensor_scalar(out=turn_row[:, :, 1, :], in0=turn_row[:, :, 0, :], scalar1=-1.0, scalar2=None, op0=ALU.mult)
-        pos = keep.tile([P, S], F32, name="pos")
+        pos = keep.tile([P, S // P], F32, name="pos")
         nc.gpsimd.iota(
-            pos[:].rearrange("p (i a q) -> p i a q", a=SUB, q=P),
-            pattern=[[TOK, S // TOK], [1, SUB], [SUB, P]],
+            pos[:].rearrange("p (i a) -> p i a", a=SUB),
+            pattern=[[TOK, S // TOK], [1, SUB]],
             base=0,
-            channel_multiplier=0,
+            channel_multiplier=SUB,
             allow_small_or_imprecise_dtypes=True,
         )
+        turns = keep.tile([P, S // P, NF], F32, name="turns")
+        for j in range(NF):
+            nc.gpsimd.tensor_scalar(
+                out=turns[:, :, j], in0=pos[:], scalar1=10000.0 ** (-j / NF) / (2.0 * math.pi), scalar2=None, op0=ALU.mult
+            )
+        whole = keep.tile([P, S // P, NF], I32, name="whole")
+        frac = keep.tile([P, S // P, NF], F32, name="frac")
+        table = {name: keep.tile([P, S], F32, name=f"{name}_table") for name in ("cos", "sin")}
         bd = keep.tile([P, G, PACK], F32, name="bd")
         bu = keep.tile([P, 1], F32, name="bu")
         br = keep.tile([P, 1], F32, name="br")
@@ -99,98 +101,102 @@ def tile_multiheadlatentattention_pa_t_kernel(
         nc.gpsimd.tensor_copy(out=bu[:], in_=bu16[:])
         nc.gpsimd.tensor_copy(out=br[:], in_=br16[:])
 
-        xs, xt, xg, xq, xqs = {}, {}, {}, {}, {}
+        xs, xg, xq, xqs = {}, {}, {}, {}
         wg, wq, wqs = {}, {}, {}
         qp, qg, qq, qqs = {}, {}, {}, {}
         acc2, o1, m1, m2, osb = {}, {}, {}, {}, {}
-
-        def widen(i, part):
-            if part == 0:
-                xs[i] = work.tile([P, SUB, D], BF16, name="xs", bufs=3, align_bytes=64)
-            two = slice(2 * part, 2 * part + 2)
-            nc.scalar.copy(out=xs[i][:, two, :], in_=xb[i][:, two, :].bitcast(FP8))
-
-        def turn(i, a):
-            xt[i, a] = psum.tile([P, G, 2, P], F32, name="tp", bufs=3)
-            words = xs[i][:, a, :].bitcast(F32)
-            for g in range(G):
-                for u in range(2):
-                    nc.tensor.transpose(xt[i, a][:, g, u, :], words[:, 256 * g + u : 256 * (g + 1) : 2], ident[:])
+        width = [n * P for (blk, a0, n) in TILES]
 
         def product(i, a):
-            if a == 0:
-                xg[i] = work.tile([P, G, TOK, PACK], BF16, name="xg", align_bytes=64)
-            halves = xt[i, a][:].rearrange("p g u r -> p (g u r)").bitcast(BF16)
-            for g in range(G):
-                nc.vector.tensor_tensor(
-                    out=xg[i][:, g, a * P : (a + 1) * P, :].rearrange("p r (u e) -> p r u e", e=2),
-                    in0=halves[:, g * 512 : (g + 1) * 512].rearrange("p (u r e) -> p r u e", u=2, e=2),
-                    in1=scale[:, g : g + 1, :].to_broadcast([P, P, PACK]).rearrange("p r (u e) -> p r u e", e=2),
-                    op=ALU.mult,
-                )
+            blk, a0, n = TILES[i]
+            xs[i, a] = work.tile([P, D], BF16, name="xs", bufs=8, align_bytes=64)
+            nc.vector.tensor_tensor(out=xs[i, a][:], in0=xb[blk][:, a0 + a, :].bitcast(FP8), in1=scale[:], op=ALU.mult)
 
-        def quantize_x(i, g):
-            if g == 0:
-                xq[i] = work.tile([P, G, TOK], U32, name="xq", align_bytes=64)
-                xqs[i] = work.tile([P, G, TOK], U8, name="xqs", align_bytes=64)
+        def turn(i, a):
+            bank = psum.tile([P, G, 2, P], F32, name="tp", bufs=2)
+            words = xs[i, a][:].bitcast(F32)
+            for g in range(G):
+                for u in range(2):
+                    nc.tensor.transpose(bank[:, g, u, :], words[:, 256 * g + u : 256 * (g + 1) : 2], ident[:])
+            if a == 0:
+                xg[i] = work.tile([P, G, width[i], PACK], BF16, name="xg", align_bytes=64)
+            dst = xg[i][:].rearrange("p g n t -> p (g n t)").bitcast(F32).rearrange("p (g n u) -> p g n u", g=G, u=2)
+            nc.scalar.copy(out=dst[:, :, a * P : (a + 1) * P, :], in_=bank[:].rearrange("p g u r -> p g r u"))
+
+        def quantize_x(i):
+            xq[i] = work.tile([P, G, width[i]], U32, name="xq", align_bytes=64)
+            xqs[i] = work.tile([P, G, width[i]], U8, name="xqs", align_bytes=64)
             nc.vector.quantize_mx(
-                out=xq[i][:, g, :].bitcast(FP8X4), scales=xqs[i][:, g, :], in_=xg[i][:, g, :, :].rearrange("p n t -> p (n t)")
+                out=xq[i][:].rearrange("p g n -> p (g n)").bitcast(FP8X4),
+                scales=xqs[i][:].rearrange("p g n -> p (g n)"),
+                in_=xg[i][:].rearrange("p g n t -> p (g n t)"),
             )
 
         def group_w(g, g2, on_scalar):
-            wg[g, g2] = keep.tile([P, K_PASS, PACK], BF16, name=f"wg{g}{g2}", align_bytes=64)
-            dst = wg[g, g2][:].rearrange("p (t m) j -> p t m j", t=PACK)
+            if g == 0:
+                wg[g2] = keep.tile([P, G, K_PASS, PACK], BF16, name=f"wg{g2}", align_bytes=64)
+            dst = wg[g2][:, g, :, :].rearrange("p (t m) j -> p t m j", t=PACK)
             rows = w_raw[g, g2][:].rearrange("p j (m t) -> p t m j", t=PACK)
             if on_scalar:
                 nc.scalar.copy(out=dst, in_=rows)
             else:
                 nc.vector.tensor_copy(out=dst, in_=rows)
 
-        def quantize_w(g, g2):
-            wq[g, g2] = keep.tile([P, K_PASS], U32, name=f"wq{g}{g2}", align_bytes=64)
-            wqs[g, g2] = keep.tile([P, K_PASS], U8, name=f"wqs{g}{g2}", align_bytes=64)
+        def quantize_w(g2):
+            wq[g2] = keep.tile([P, G, K_PASS], U32, name=f"wq{g2}", align_bytes=64)
+            wqs[g2] = keep.tile([P, G, K_PASS], U8, name=f"wqs{g2}", align_bytes=64)
             nc.vector.quantize_mx(
-                out=wq[g, g2][:].bitcast(FP8X4), scales=wqs[g, g2][:], in_=wg[g, g2][:].rearrange("p n j -> p (n j)")
+                out=wq[g2][:].rearrange("p g c -> p (g c)").bitcast(FP8X4),
+                scales=wqs[g2][:].rearrange("p g c -> p (g c)"),
+                in_=wg[g2][:].rearrange("p g c j -> p (g c j)"),
             )
 
-        w2g = keep.tile([P, 2, G, QW, PACK], BF16, name="w2g", align_bytes=64)
-        w2q = keep.tile([P, 2, G, QW], U32, name="w2q", align_bytes=64)
-        w2qs = keep.tile([P, 2, G, QW], U8, name="w2qs", align_bytes=64)
-
         def latent(i, g2, slots):
+            paired = g2 == 0 and i % 2 == 0 and TILES[i][2] == SUB
             if slots[0] == 0:
-                qp[i, g2] = work.tile([P, PACK, TOK], BF16, name="qp", bufs=3, align_bytes=64)
+                qp[i, g2] = work.tile([P, PACK * width[i]], BF16, name="qp", bufs=3, align_bytes=64)
+            if paired:
+                planes = qp[i, g2][:].rearrange("p (h n e) -> p h e n", h=2, e=2)
+            else:
+                planes = qp[i, g2][:].rearrange("p (h e n) -> p h e n", h=2, e=2)
             for t in slots:
-                bank = psum.tile([P, TOK], F32, name="s1", bufs=3)
+                bank = psum.tile([P, width[i]], F32, name="s1", bufs=4)
                 for g in range(G):
                     nc.tensor.matmul_mx(
                         out=bank[:],
-                        lhsT=wq[g, g2][:, t * P : (t + 1) * P].bitcast(FP8X4),
-                        lhsT_scale=wqs[g, g2][:, t * P : (t + 1) * P],
+                        lhsT=wq[g2][:, g, t * P : (t + 1) * P].bitcast(FP8X4),
+                        lhsT_scale=wqs[g2][:, g, t * P : (t + 1) * P],
                         rhs=xq[i][:, g, :].bitcast(FP8X4),
                         rhs_scale=xqs[i][:, g, :],
                         start=(g == 0),
                         stop=(g == G - 1),
                     )
-                nc.scalar.activation(out=qp[i, g2][:, t, :], in_=bank[:], func=ACT.Identity, bias=bd[:, g2, t : t + 1])
+                nc.scalar.activation(out=planes[:, t // 2, t % 2, :], in_=bank[:], func=ACT.Identity, bias=bd[:, g2, t : t + 1])
 
         def group_q(i, g2):
-            qg[i, g2] = work.tile([P, TOK, PACK], BF16, name="qg", bufs=3, align_bytes=64)
-            nc.vector.tensor_copy(
-                out=qg[i, g2][:].rearrange("p (c n) t -> p c t n", n=4), in_=qp[i, g2][:].rearrange("p t (c n) -> p c t n", n=4)
-            )
+            qg[i, g2] = work.tile([P, width[i], PACK], BF16, name="qg", bufs=3, align_bytes=64)
+            if g2 == 0 and i % 2 == 0 and TILES[i][2] == SUB:
+                nc.vector.tensor_copy(
+                    out=qg[i, g2][:].rearrange("p n t -> p (n t)").bitcast(F32).rearrange("p (n h) -> p n h", h=2),
+                    in_=qp[i, g2][:].bitcast(F32).rearrange("p (h n) -> p n h", h=2),
+                )
+            else:
+                nc.vector.tensor_copy(
+                    out=qg[i, g2][:].rearrange("p (c n) t -> p c t n", n=4),
+                    in_=qp[i, g2][:].rearrange("p (t c n) -> p c t n", t=PACK, n=4),
+                )
 
         def quantize_q(i, g2):
             if g2 == 0:
-                qq[i] = work.tile([P, G, TOK], U32, name="qq", align_bytes=64)
-                qqs[i] = work.tile([P, G, TOK], U8, name="qqs", align_bytes=64)
+                qq[i] = work.tile([P, G, width[i]], U32, name="qq", align_bytes=64)
+                qqs[i] = work.tile([P, G, width[i]], U8, name="qqs", align_bytes=64)
             nc.vector.quantize_mx(
                 out=qq[i][:, g2, :].bitcast(FP8X4), scales=qqs[i][:, g2, :], in_=qg[i, g2][:].rearrange("p n t -> p (n t)")
             )
 
         def heads(i):
             for s in range(2):
-                acc2[i, s] = psum.tile([P, TOK], F32, name=f"s2{s}")
+                acc2[i, s] = psum.tile([P, width[i]], F32, name=f"s2{s}")
                 for g in range(G):
                     nc.tensor.matmul_mx(
                         out=acc2[i, s][:],
@@ -202,130 +208,169 @@ def tile_multiheadlatentattention_pa_t_kernel(
                         stop=(g == G - 1),
                     )
 
+        def rope(i):
+            blk, a0, n = TILES[i]
+            first = (blk % (S // TOK)) * TOK + a0 * P
+            cols = slice(first, first + width[i])
+            m1[i] = work.tile([P, width[i]], F32, name="m1")
+            m2[i] = work.tile([P, width[i]], F32, name="m2")
+            nc.vector.scalar_tensor_tensor(out=m1[i][:], in0=acc2[i, 1][:], scalar=br[:], in1=table["cos"][:, cols], op0=ALU.add, op1=ALU.mult)
+            nc.vector.scalar_tensor_tensor(out=m2[i][:], in0=acc2[i, 1][:], scalar=br[:], in1=table["sin"][:, cols], op0=ALU.add, op1=ALU.mult)
+
         def head1(i):
-            o1[i] = work.tile([P, TOK], F32, name="o1")
+            o1[i] = work.tile([P, width[i]], F32, name="o1")
             nc.scalar.activation(out=o1[i][:], in_=acc2[i, 0][:], func=ACT.Identity, bias=bu[:])
 
-        def rope(i):
-            cols = slice((i % 2) * TOK, (i % 2 + 1) * TOK)
-            m1[i] = work.tile([P, TOK], F32, name="m1")
-            m2[i] = work.tile([P, TOK], F32, name="m2")
-            nc.vector.scalar_tensor_tensor(out=m1[i][:], in0=acc2[i, 1][:], scalar=br[:], in1=cos[:, cols], op0=ALU.add, op1=ALU.mult)
-            nc.vector.scalar_tensor_tensor(out=m2[i][:], in0=acc2[i, 1][:], scalar=br[:], in1=sin[:, cols], op0=ALU.add, op1=ALU.mult)
-
-        def finish(i):
-            osb[i] = work.tile([P, SUB, 2 * QW], F32, name="osb")
-            for half in range(2):
-                bank = psum.tile([P, 2, 2 * QW], F32, name="tp", bufs=3)
-                for r in range(2):
-                    a = 2 * half + r
-                    cols = slice(a * P, (a + 1) * P)
-                    nc.tensor.transpose(bank[:, r, 0:QW], o1[i][:, cols], ident[:])
-                    nc.tensor.matmul(bank[:, r, QW : 2 * QW], lhsT=m1[i][:, cols], rhs=ident[:], start=True, stop=False, is_transpose=True)
-                    nc.tensor.matmul(
-                        bank[:, r, QW : 2 * QW],
-                        lhsT=m2[i][:, cols],
-                        rhs=swap[:].rearrange("p h e j -> p (h e j)"),
-                        start=False,
-                        stop=True,
-                        is_transpose=True,
-                    )
-                nc.scalar.copy(
-                    out=osb[i][:, 2 * half : 2 * half + 2, :].rearrange("p r (h s d) -> p r s h d", h=H, s=2),
-                    in_=bank[:].rearrange("p r (s h d) -> p r s h d", s=2, h=H),
+        def finish(i, half):
+            blk, a0, n = TILES[i]
+            if half == 0:
+                osb[i] = work.tile([P, n, 2 * QW], F32, name="osb")
+            bank = psum.tile([P, 2, 2 * QW], F32, name="tp", bufs=2)
+            two = slice(2 * half, 2 * half + 2)
+            for r in range(2):
+                cols = slice((2 * half + r) * P, (2 * half + r + 1) * P)
+                nc.tensor.transpose(bank[:, r, 0:QW], o1[i][:, cols], ident[:])
+                nc.tensor.matmul(bank[:, r, QW : 2 * QW], lhsT=m1[i][:, cols], rhs=ident[:], start=True, stop=False, is_transpose=True)
+                nc.tensor.matmul(
+                    bank[:, r, QW : 2 * QW],
+                    lhsT=m2[i][:, cols],
+                    rhs=swap[:].rearrange("p h e j -> p (h e j)"),
+                    start=False,
+                    stop=True,
+                    is_transpose=True,
                 )
-                nc.sync.dma_start(out=out_rows[i][:, 2 * half : 2 * half + 2, :], in_=osb[i][:, 2 * half : 2 * half + 2, :])
+            nc.scalar.copy(
+                out=osb[i][:, two, :].rearrange("p r (h s d) -> p r s h d", h=H, s=2),
+                in_=bank[:].rearrange("p r (s h d) -> p r s h d", s=2, h=H),
+            )
+            nc.sync.dma_start(out=out_rows[blk][:, a0 + 2 * half : a0 + 2 * half + 2, :], in_=osb[i][:, two, :])
 
-        widen(0, 0)
-        widen(0, 1)
-        group_w(0, 0, True)
-        for a in range(3):
-            turn(0, a)
+        scale = keep.tile([P, D], F32, name="scale")
+        scale_nc = scale[:].rearrange("p (n c) -> p n c", n=P)
+        for half in range(2):
+            bank = psum.tile([P, D // P // 2, P], F32, name=f"s2{half}")
+            four = slice(4 * half, 4 * half + 4)
+            for c in range(4):
+                nc.tensor.transpose(bank[:, c, :], scale_col[:, 4 * half + c : 4 * half + c + 1].to_broadcast([P, P]), ident[:])
+            if half == 0:
+                nc.vector.tensor_copy(out=scale_nc[:, :, four], in_=bank[:].rearrange("p c n -> p n c"))
+            else:
+                nc.scalar.copy(out=scale_nc[:, :, four], in_=bank[:].rearrange("p c n -> p n c"))
         product(0, 0)
         product(0, 1)
-        turn(0, 3)
-        group_w(1, 0, False)
-        product(0, 2)
-        quantize_w(0, 0)
-        product(0, 3)
-        quantize_w(1, 0)
-        quantize_x(0, 0)
-        quantize_x(0, 1)
-        group_w(0, 1, True)
-        group_w(1, 1, False)
-        widen(1, 0)
-        widen(1, 1)
-        quantize_w(0, 1)
-        quantize_w(1, 1)
-        nc.vector.tensor_copy(
-            out=w2g[:].rearrange("p s g n j -> p (s g) n j"), in_=w2_raw[:].rearrange("p s g j n -> p (s g) n j")
-        )
-
-        freq_bank = psum.tile([P, P], F32, name="s20")
-        nc.tensor.transpose(freq_bank[:], turn_row[:].rearrange("p h e j -> p (h e j)"), ident[:])
-        freq = keep.tile([P, 1], F32, name="freq")
-        nc.scalar.copy(out=freq[:], in_=freq_bank[:, 0:1])
-        turns = keep.tile([P, S], F32, name="turns")
-        whole = keep.tile([P, S], I32, name="whole")
-        frac = keep.tile([P, S], F32, name="frac")
-        sin = keep.tile([P, S], F32, name="sin")
-        cos = keep.tile([P, S], F32, name="cos")
-        half_sin = keep.tile([P, S], F32, name="half_sin")
-        nc.scalar.activation(out=turns[:], in_=pos[:], func=ACT.Copy, scale=freq[:])
         nc.vector.tensor_copy(out=whole[:], in_=turns[:])
         nc.vector.scalar_tensor_tensor(out=frac[:], in0=whole[:], scalar=-1.0, in1=turns[:], op0=ALU.mult, op1=ALU.add)
-        nc.scalar.activation(out=sin[:], in_=frac[:], func=ACT.Sin, scale=2.0 * math.pi)
+        sin_small = keep.tile([P, S // P, 1, NF], F32, name="sin_small")
+        cos_small = keep.tile([P, S // P, 1, NF], F32, name="cos_small")
+        half_sin = keep.tile([P, S // P, NF], F32, name="half_sin")
+        nc.scalar.activation(out=sin_small[:, :, 0, :], in_=frac[:], func=ACT.Sin, scale=2.0 * math.pi)
         nc.scalar.activation(out=half_sin[:], in_=frac[:], func=ACT.Sin, scale=math.pi)
-        nc.gpsimd.tensor_tensor(out=cos[:], in0=half_sin[:], in1=half_sin[:], op=ALU.mult)
-        nc.gpsimd.tensor_scalar(out=cos[:], in0=cos[:], scalar1=-2.0, scalar2=1.0, op0=ALU.mult, op1=ALU.add)
+        nc.gpsimd.tensor_tensor(out=half_sin[:], in0=half_sin[:], in1=half_sin[:], op=ALU.mult)
+        nc.gpsimd.tensor_scalar(out=cos_small[:, :, 0, :], in0=half_sin[:], scalar1=-2.0, scalar2=1.0, op0=ALU.mult, op1=ALU.add)
+        group_w(0, 0, True)
+        turn(0, 0)
+        turn(0, 1)
+        group_w(1, 0, False)
+        quantize_w(0)
+        quantize_x(0)
+        group_w(0, 1, True)
+        product(1, 0)
+        product(1, 1)
+        w2g = keep.tile([P, 2, G, QW, PACK], BF16, name="w2g", align_bytes=64)
+        w2q = keep.tile([P, 2, G, QW], U32, name="w2q", align_bytes=64)
+        w2qs = keep.tile([P, 2, G, QW], U8, name="w2qs", align_bytes=64)
 
-        nc.vector.quantize_mx(
-            out=w2q[:].rearrange("p s g n -> p (s g n)").bitcast(FP8X4),
-            scales=w2qs[:].rearrange("p s g n -> p (s g n)"),
-            in_=w2g[:].rearrange("p s g n j -> p (s g n j)"),
-        )
+        def spread(name):
+            for half in range(2):
+                bank = psum.tile([P, SUB, P], F32, name=f"s2{half}")
+                for a in range(SUB):
+                    nc.tensor.transpose(bank[:, a, :], wide[name][:, half * SUB + a, :, :].rearrange("p h j -> p (h j)"), ident[:])
+                nc.scalar.copy(out=table[name][:, half * TOK : (half + 1) * TOK], in_=bank[:].rearrange("p a q -> p (a q)"))
 
-        for i in range(TILES + 2):
-            ahead = i + 2 < TILES
-            turn_on = i + 1 < TILES
-            latent_on = i < TILES
-            head_on = 1 <= i <= TILES
-            if latent_on:
-                latent(i, 0, (0, 1))
-            if turn_on:
+        def group_w2():
+            nc.scalar.copy(
+                out=w2g[:].rearrange("p s g n j -> p (s g) n j"), in_=w2_raw[:].rearrange("p s g j n -> p (s g) n j")
+            )
+
+        def quantize_w2():
+            nc.vector.quantize_mx(
+                out=w2q[:].rearrange("p s g n -> p (s g n)").bitcast(FP8X4),
+                scales=w2qs[:].rearrange("p s g n -> p (s g n)"),
+                in_=w2g[:].rearrange("p s g n j -> p (s g n j)"),
+            )
+
+        wide = {}
+
+        def widen_tables():
+            wide["cos"] = keep.tile([P, S // P, 2 * H, NF], F32, name="cos_wide")
+            nc.vector.tensor_copy(out=wide["cos"][:], in_=cos_small[:].to_broadcast([P, S // P, 2 * H, NF]))
+            wide["sin"] = keep.tile([P, S // P, 2 * H, NF], F32, name="sin_wide")
+            sin_heads = wide["sin"][:].rearrange("p i (h e) j -> p i h e j", e=2)
+            sin_again = sin_small[:].to_broadcast([P, S // P, H, NF])
+            nc.vector.tensor_copy(out=sin_heads[:, :, :, 0, :], in_=sin_again)
+            nc.vector.tensor_scalar(out=sin_heads[:, :, :, 1, :], in0=sin_again, scalar1=-1.0, scalar2=None, op0=ALU.mult)
+
+        count = len(TILES)
+        for i in range(count + 2):
+            here = i < count
+            head = 1 <= i <= count
+            last = i >= 2
+            turns_next = TILES[i + 1][2] if i + 1 < count else 0
+            products_next = TILES[i + 2][2] if i + 2 < count else 0
+
+            if turns_next:
                 turn(i + 1, 0)
-                turn(i + 1, 1)
-                product(i + 1, 0)
-            if head_on:
+            if here:
+                latent(i, 0, (0, 1))
+            if i == 0:
+                group_w(1, 1, False)
+            if i == 1:
+                quantize_w2()
+            if head:
                 group_q(i - 1, 1)
-            if latent_on:
+            if products_next:
+                product(i + 2, 0)
+
+            if turns_next:
+                turn(i + 1, 1)
+            if here:
                 latent(i, 0, (2, 3))
-            if turn_on:
-                product(i + 1, 1)
-                turn(i + 1, 2)
-                turn(i + 1, 3)
-            if head_on:
+            if i == 0:
+                quantize_w(1)
+            if last:
+                rope(i - 2)
+            if head:
                 quantize_q(i - 1, 1)
-            if ahead:
-                widen(i + 2, 0)
-            if turn_on:
-                product(i + 1, 2)
-            if latent_on:
+            if products_next:
+                product(i + 2, 1)
+
+            if turns_next == SUB:
+                turn(i + 1, 2)
+            if here:
                 latent(i, 1, (0, 1))
-                group_q(i, 0)
-            if turn_on:
-                product(i + 1, 3)
-            if i >= 2:
-                finish(i - 2)
-            if ahead:
-                widen(i + 2, 1)
-            if latent_on:
-                quantize_q(i, 0)
+
+            if turns_next == SUB:
+                turn(i + 1, 3)
+            if here:
                 latent(i, 1, (2, 3))
-            if turn_on:
-                quantize_x(i + 1, 0)
-                quantize_x(i + 1, 1)
-            if head_on:
+            if last:
+                for half in range(TILES[i - 2][2] // 2):
+                    finish(i - 2, half)
+            if head:
                 heads(i - 1)
                 head1(i - 1)
-                rope(i - 1)
+            if products_next == SUB:
+                product(i + 2, 2)
+            if turns_next:
+                quantize_x(i + 1)
+            if here:
+                group_q(i, 0)
+            if products_next == SUB:
+                product(i + 2, 3)
+            if here:
+                quantize_q(i, 0)
+            if i == 0:
+                group_w2()
+                widen_tables()
+                spread("cos")
+                spread("sin")

import math
from contextlib import ExitStack

import concourse.mybir as mybir
from concourse.masks import make_identity

F32 = mybir.dt.float32
BF16 = mybir.dt.bfloat16
I32 = mybir.dt.int32
U32 = mybir.dt.uint32
U8 = mybir.dt.uint8
FP8 = mybir.dt.float8_e4m3fn
FP8X4 = mybir.dt.float8_e4m3fn_x4
ACT = mybir.ActivationFunctionType
ALU = mybir.AluOpType

P = 128
B, S, D, L = 4, 1024, 1024, 1024
H, HALF = 4, 32
NF = HALF // 2
QW = H * HALF
PACK = 4
K_PASS = P * PACK
G = D // K_PASS
TOK = 512
SUB = TOK // P
BLOCKS = B * S // TOK
TILES = [(0, 0, 2), (0, 2, 2)] + [(i, 0, SUB) for i in range(1, BLOCKS - 1)] + [(BLOCKS - 1, 0, 2), (BLOCKS - 1, 2, 2)]
FLOPS = 2 * B * S * D * L + 2 * B * S * L * 2 * QW


def tile_multiheadlatentattention_pa_t_kernel(
    tc, x_bytes, x_scale, W_q_d, b_q_d, W_q_u, b_q_u, W_rq, b_rq, out
):
    nc = tc.nc
    x_rows = x_bytes.rearrange("b (i p a) k -> (b i) p a k", p=P, a=SUB)
    out_rows = out.rearrange("b (i p a) h d -> (b i) p a (h d)", p=P, a=SUB)

    with ExitStack() as ctx:
        keep = ctx.enter_context(tc.tile_pool(name="keep", bufs=1))
        work = ctx.enter_context(tc.tile_pool(name="work", bufs=2))
        psum = ctx.enter_context(tc.psum_pool(name="psum", bufs=1))
        ctx.enter_context(tc.manual_schedule())

        scale_col = keep.tile([P, D // P], F32, name="scale_col")
        nc.sync.dma_start(out=scale_col[:], in_=x_scale.rearrange("o u (n c) -> n (o u c)", n=P))
        xb = [keep.tile([P, SUB, D], U8, name=f"xb{i}") for i in range(BLOCKS)]
        nc.sync.dma_start(out=xb[0][:, 0:2, :], in_=x_rows[0][:, 0:2, :])
        w_raw = {}
        for g2 in range(G):
            for g in range(G):
                w_raw[g, g2] = keep.tile([P, PACK, K_PASS], BF16, name=f"wraw{g}{g2}")
                nc.sync.dma_start(
                    out=w_raw[g, g2][:],
                    in_=W_q_d[g * K_PASS : (g + 1) * K_PASS, g2 * K_PASS : (g2 + 1) * K_PASS].rearrange("(p j) c -> p j c", j=PACK),
                )
            if g2 == 0:
                nc.sync.dma_start(out=xb[0][:, 2:4, :], in_=x_rows[0][:, 2:4, :])
        nc.sync.dma_start(out=xb[1][:], in_=x_rows[1])
        w2_raw = keep.tile([P, 2, G, PACK, QW], BF16, name="w2raw")
        for s, w in enumerate((W_q_u, W_rq)):
            for g in range(G):
                nc.sync.dma_start(out=w2_raw[:, s, g, :, :], in_=w[g * K_PASS : (g + 1) * K_PASS, :].rearrange("(p j) c -> p j c", j=PACK))
        for i in range(2, BLOCKS):
            nc.sync.dma_start(out=xb[i][:], in_=x_rows[i])

        bd16 = keep.tile([P, G, PACK], BF16, name="bd16")
        bu16 = keep.tile([P, 1], BF16, name="bu16")
        br16 = keep.tile([P, 1], BF16, name="br16")
        nc.scalar.dma_start(out=bd16[:], in_=b_q_d.rearrange("(g p t) -> p g t", p=P, t=PACK))
        nc.scalar.dma_start(out=bu16[:], in_=b_q_u.rearrange("(p o) -> p o", o=1))
        nc.scalar.dma_start(out=br16[:], in_=b_rq.rearrange("(p o) -> p o", o=1))

        ident = keep.tile([P, P], F32, name="ident")
        make_identity(nc, ident[:])
        swap = keep.tile([P, H, 2, NF], F32, name="swap")
        ident_h = ident[:].rearrange("p (h e j) -> p h e j", h=H, e=2)
        nc.gpsimd.tensor_copy(out=swap[:, :, 0, :], in_=ident_h[:, :, 1, :])
        nc.gpsimd.tensor_copy(out=swap[:, :, 1, :], in_=ident_h[:, :, 0, :])

        pos = keep.tile([P, S // P], F32, name="pos")
        nc.gpsimd.iota(
            pos[:].rearrange("p (i a) -> p i a", a=SUB),
            pattern=[[TOK, S // TOK], [1, SUB]],
            base=0,
            channel_multiplier=SUB,
            allow_small_or_imprecise_dtypes=True,
        )
        turns = keep.tile([P, S // P, NF], F32, name="turns")
        for j in range(NF):
            nc.gpsimd.tensor_scalar(
                out=turns[:, :, j], in0=pos[:], scalar1=10000.0 ** (-j / NF) / (2.0 * math.pi), scalar2=None, op0=ALU.mult
            )
        whole = keep.tile([P, S // P, NF], I32, name="whole")
        frac = keep.tile([P, S // P, NF], F32, name="frac")
        table = {name: keep.tile([P, S], F32, name=f"{name}_table") for name in ("cos", "sin")}
        bd = keep.tile([P, G, PACK], F32, name="bd")
        bu = keep.tile([P, 1], F32, name="bu")
        br = keep.tile([P, 1], F32, name="br")
        nc.gpsimd.tensor_copy(out=bd[:], in_=bd16[:])
        nc.gpsimd.tensor_copy(out=bu[:], in_=bu16[:])
        nc.gpsimd.tensor_copy(out=br[:], in_=br16[:])

        xs, xg, xq, xqs = {}, {}, {}, {}
        wg, wq, wqs = {}, {}, {}
        qp, qg, qq, qqs = {}, {}, {}, {}
        acc2, o1, m1, m2, osb = {}, {}, {}, {}, {}
        width = [n * P for (blk, a0, n) in TILES]

        def product(i, a):
            blk, a0, n = TILES[i]
            xs[i, a] = work.tile([P, D], BF16, name="xs", bufs=8, align_bytes=64)
            nc.vector.tensor_tensor(out=xs[i, a][:], in0=xb[blk][:, a0 + a, :].bitcast(FP8), in1=scale[:], op=ALU.mult)

        def turn(i, a):
            bank = psum.tile([P, G, 2, P], F32, name="tp", bufs=2)
            words = xs[i, a][:].bitcast(F32)
            for g in range(G):
                for u in range(2):
                    nc.tensor.transpose(bank[:, g, u, :], words[:, 256 * g + u : 256 * (g + 1) : 2], ident[:])
            if a == 0:
                xg[i] = work.tile([P, G, width[i], PACK], BF16, name="xg", align_bytes=64)
            dst = xg[i][:].rearrange("p g n t -> p (g n t)").bitcast(F32).rearrange("p (g n u) -> p g n u", g=G, u=2)
            nc.scalar.copy(out=dst[:, :, a * P : (a + 1) * P, :], in_=bank[:].rearrange("p g u r -> p g r u"))

        def quantize_x(i):
            xq[i] = work.tile([P, G, width[i]], U32, name="xq", align_bytes=64)
            xqs[i] = work.tile([P, G, width[i]], U8, name="xqs", align_bytes=64)
            nc.vector.quantize_mx(
                out=xq[i][:].rearrange("p g n -> p (g n)").bitcast(FP8X4),
                scales=xqs[i][:].rearrange("p g n -> p (g n)"),
                in_=xg[i][:].rearrange("p g n t -> p (g n t)"),
            )

        def group_w(g, g2, on_scalar):
            if g == 0:
                wg[g2] = keep.tile([P, G, K_PASS, PACK], BF16, name=f"wg{g2}", align_bytes=64)
            dst = wg[g2][:, g, :, :].rearrange("p (t m) j -> p t m j", t=PACK)
            rows = w_raw[g, g2][:].rearrange("p j (m t) -> p t m j", t=PACK)
            if on_scalar:
                nc.scalar.copy(out=dst, in_=rows)
            else:
                nc.vector.tensor_copy(out=dst, in_=rows)

        def quantize_w(g2):
            wq[g2] = keep.tile([P, G, K_PASS], U32, name=f"wq{g2}", align_bytes=64)
            wqs[g2] = keep.tile([P, G, K_PASS], U8, name=f"wqs{g2}", align_bytes=64)
            nc.vector.quantize_mx(
                out=wq[g2][:].rearrange("p g c -> p (g c)").bitcast(FP8X4),
                scales=wqs[g2][:].rearrange("p g c -> p (g c)"),
                in_=wg[g2][:].rearrange("p g c j -> p (g c j)"),
            )

        def latent(i, g2, slots):
            paired = g2 == 0 and i % 2 == 0 and TILES[i][2] == SUB
            if slots[0] == 0:
                qp[i, g2] = work.tile([P, PACK * width[i]], BF16, name="qp", bufs=3, align_bytes=64)
            if paired:
                planes = qp[i, g2][:].rearrange("p (h n e) -> p h e n", h=2, e=2)
            else:
                planes = qp[i, g2][:].rearrange("p (h e n) -> p h e n", h=2, e=2)
            for t in slots:
                bank = psum.tile([P, width[i]], F32, name="s1", bufs=4)
                for g in range(G):
                    nc.tensor.matmul_mx(
                        out=bank[:],
                        lhsT=wq[g2][:, g, t * P : (t + 1) * P].bitcast(FP8X4),
                        lhsT_scale=wqs[g2][:, g, t * P : (t + 1) * P],
                        rhs=xq[i][:, g, :].bitcast(FP8X4),
                        rhs_scale=xqs[i][:, g, :],
                        start=(g == 0),
                        stop=(g == G - 1),
                    )
                nc.scalar.activation(out=planes[:, t // 2, t % 2, :], in_=bank[:], func=ACT.Identity, bias=bd[:, g2, t : t + 1])

        def group_q(i, g2):
            qg[i, g2] = work.tile([P, width[i], PACK], BF16, name="qg", bufs=3, align_bytes=64)
            if g2 == 0 and i % 2 == 0 and TILES[i][2] == SUB:
                nc.vector.tensor_copy(
                    out=qg[i, g2][:].rearrange("p n t -> p (n t)").bitcast(F32).rearrange("p (n h) -> p n h", h=2),
                    in_=qp[i, g2][:].bitcast(F32).rearrange("p (h n) -> p n h", h=2),
                )
            else:
                nc.vector.tensor_copy(
                    out=qg[i, g2][:].rearrange("p (c n) t -> p c t n", n=4),
                    in_=qp[i, g2][:].rearrange("p (t c n) -> p c t n", t=PACK, n=4),
                )

        def quantize_q(i, g2):
            if g2 == 0:
                qq[i] = work.tile([P, G, width[i]], U32, name="qq", align_bytes=64)
                qqs[i] = work.tile([P, G, width[i]], U8, name="qqs", align_bytes=64)
            nc.vector.quantize_mx(
                out=qq[i][:, g2, :].bitcast(FP8X4), scales=qqs[i][:, g2, :], in_=qg[i, g2][:].rearrange("p n t -> p (n t)")
            )

        def heads(i):
            for s in range(2):
                acc2[i, s] = psum.tile([P, width[i]], F32, name=f"s2{s}")
                for g in range(G):
                    nc.tensor.matmul_mx(
                        out=acc2[i, s][:],
                        lhsT=w2q[:, s, g, :].bitcast(FP8X4),
                        lhsT_scale=w2qs[:, s, g, :],
                        rhs=qq[i][:, g, :].bitcast(FP8X4),
                        rhs_scale=qqs[i][:, g, :],
                        start=(g == 0),
                        stop=(g == G - 1),
                    )

        def rope(i):
            blk, a0, n = TILES[i]
            first = (blk % (S // TOK)) * TOK + a0 * P
            cols = slice(first, first + width[i])
            m1[i] = work.tile([P, width[i]], F32, name="m1")
            m2[i] = work.tile([P, width[i]], F32, name="m2")
            nc.vector.scalar_tensor_tensor(out=m1[i][:], in0=acc2[i, 1][:], scalar=br[:], in1=table["cos"][:, cols], op0=ALU.add, op1=ALU.mult)
            nc.vector.scalar_tensor_tensor(out=m2[i][:], in0=acc2[i, 1][:], scalar=br[:], in1=table["sin"][:, cols], op0=ALU.add, op1=ALU.mult)

        def head1(i):
            o1[i] = work.tile([P, width[i]], F32, name="o1")
            nc.scalar.activation(out=o1[i][:], in_=acc2[i, 0][:], func=ACT.Identity, bias=bu[:])

        def finish(i, half):
            blk, a0, n = TILES[i]
            if half == 0:
                osb[i] = work.tile([P, n, 2 * QW], F32, name="osb")
            bank = psum.tile([P, 2, 2 * QW], F32, name="tp", bufs=2)
            two = slice(2 * half, 2 * half + 2)
            for r in range(2):
                cols = slice((2 * half + r) * P, (2 * half + r + 1) * P)
                nc.tensor.transpose(bank[:, r, 0:QW], o1[i][:, cols], ident[:])
                nc.tensor.matmul(bank[:, r, QW : 2 * QW], lhsT=m1[i][:, cols], rhs=ident[:], start=True, stop=False, is_transpose=True)
                nc.tensor.matmul(
                    bank[:, r, QW : 2 * QW],
                    lhsT=m2[i][:, cols],
                    rhs=swap[:].rearrange("p h e j -> p (h e j)"),
                    start=False,
                    stop=True,
                    is_transpose=True,
                )
            nc.scalar.copy(
                out=osb[i][:, two, :].rearrange("p r (h s d) -> p r s h d", h=H, s=2),
                in_=bank[:].rearrange("p r (s h d) -> p r s h d", s=2, h=H),
            )
            nc.sync.dma_start(out=out_rows[blk][:, a0 + 2 * half : a0 + 2 * half + 2, :], in_=osb[i][:, two, :])

        scale = keep.tile([P, D], F32, name="scale")
        scale_nc = scale[:].rearrange("p (n c) -> p n c", n=P)
        for half in range(2):
            bank = psum.tile([P, D // P // 2, P], F32, name=f"s2{half}")
            four = slice(4 * half, 4 * half + 4)
            for c in range(4):
                nc.tensor.transpose(bank[:, c, :], scale_col[:, 4 * half + c : 4 * half + c + 1].to_broadcast([P, P]), ident[:])
            if half == 0:
                nc.vector.tensor_copy(out=scale_nc[:, :, four], in_=bank[:].rearrange("p c n -> p n c"))
            else:
                nc.scalar.copy(out=scale_nc[:, :, four], in_=bank[:].rearrange("p c n -> p n c"))
        product(0, 0)
        product(0, 1)
        nc.vector.tensor_copy(out=whole[:], in_=turns[:])
        nc.vector.scalar_tensor_tensor(out=frac[:], in0=whole[:], scalar=-1.0, in1=turns[:], op0=ALU.mult, op1=ALU.add)
        sin_small = keep.tile([P, S // P, 1, NF], F32, name="sin_small")
        cos_small = keep.tile([P, S // P, 1, NF], F32, name="cos_small")
        half_sin = keep.tile([P, S // P, NF], F32, name="half_sin")
        nc.scalar.activation(out=sin_small[:, :, 0, :], in_=frac[:], func=ACT.Sin, scale=2.0 * math.pi)
        nc.scalar.activation(out=half_sin[:], in_=frac[:], func=ACT.Sin, scale=math.pi)
        nc.gpsimd.tensor_tensor(out=half_sin[:], in0=half_sin[:], in1=half_sin[:], op=ALU.mult)
        nc.gpsimd.tensor_scalar(out=cos_small[:, :, 0, :], in0=half_sin[:], scalar1=-2.0, scalar2=1.0, op0=ALU.mult, op1=ALU.add)
        group_w(0, 0, True)
        turn(0, 0)
        turn(0, 1)
        group_w(1, 0, False)
        quantize_w(0)
        quantize_x(0)
        group_w(0, 1, True)
        product(1, 0)
        product(1, 1)
        w2g = keep.tile([P, 2, G, QW, PACK], BF16, name="w2g", align_bytes=64)
        w2q = keep.tile([P, 2, G, QW], U32, name="w2q", align_bytes=64)
        w2qs = keep.tile([P, 2, G, QW], U8, name="w2qs", align_bytes=64)

        def spread(name):
            for half in range(2):
                bank = psum.tile([P, SUB, P], F32, name=f"s2{half}")
                for a in range(SUB):
                    nc.tensor.transpose(bank[:, a, :], wide[name][:, half * SUB + a, :, :].rearrange("p h j -> p (h j)"), ident[:])
                nc.scalar.copy(out=table[name][:, half * TOK : (half + 1) * TOK], in_=bank[:].rearrange("p a q -> p (a q)"))

        def group_w2():
            nc.scalar.copy(
                out=w2g[:].rearrange("p s g n j -> p (s g) n j"), in_=w2_raw[:].rearrange("p s g j n -> p (s g) n j")
            )

        def quantize_w2():
            nc.vector.quantize_mx(
                out=w2q[:].rearrange("p s g n -> p (s g n)").bitcast(FP8X4),
                scales=w2qs[:].rearrange("p s g n -> p (s g n)"),
                in_=w2g[:].rearrange("p s g n j -> p (s g n j)"),
            )

        wide = {}

        def widen_tables():
            wide["cos"] = keep.tile([P, S // P, 2 * H, NF], F32, name="cos_wide")
            nc.vector.tensor_copy(out=wide["cos"][:], in_=cos_small[:].to_broadcast([P, S // P, 2 * H, NF]))
            wide["sin"] = keep.tile([P, S // P, 2 * H, NF], F32, name="sin_wide")
            sin_heads = wide["sin"][:].rearrange("p i (h e) j -> p i h e j", e=2)
            sin_again = sin_small[:].to_broadcast([P, S // P, H, NF])
            nc.vector.tensor_copy(out=sin_heads[:, :, :, 0, :], in_=sin_again)
            nc.vector.tensor_scalar(out=sin_heads[:, :, :, 1, :], in0=sin_again, scalar1=-1.0, scalar2=None, op0=ALU.mult)

        count = len(TILES)
        for i in range(count + 2):
            here = i < count
            head = 1 <= i <= count
            last = i >= 2
            turns_next = TILES[i + 1][2] if i + 1 < count else 0
            products_next = TILES[i + 2][2] if i + 2 < count else 0

            if turns_next:
                turn(i + 1, 0)
            if here:
                latent(i, 0, (0, 1))
            if i == 0:
                group_w(1, 1, False)
            if i == 1:
                quantize_w2()
            if head:
                group_q(i - 1, 1)
            if products_next:
                product(i + 2, 0)

            if turns_next:
                turn(i + 1, 1)
            if here:
                latent(i, 0, (2, 3))
            if i == 0:
                quantize_w(1)
            if last:
                rope(i - 2)
            if head:
                quantize_q(i - 1, 1)
            if products_next:
                product(i + 2, 1)

            if turns_next == SUB:
                turn(i + 1, 2)
            if here:
                latent(i, 1, (0, 1))

            if turns_next == SUB:
                turn(i + 1, 3)
            if here:
                latent(i, 1, (2, 3))
            if last:
                for half in range(TILES[i - 2][2] // 2):
                    finish(i - 2, half)
            if head:
                heads(i - 1)
                head1(i - 1)
            if products_next == SUB:
                product(i + 2, 2)
            if turns_next:
                quantize_x(i + 1)
            if here:
                group_q(i, 0)
            if products_next == SUB:
                product(i + 2, 3)
            if here:
                quantize_q(i, 0)
            if i == 0:
                group_w2()
                widen_tables()
                spread("cos")
                spread("sin")
